import numpy as np
import ml_dtypes


def mxq(x, axis, fmt="e4m3"):
    dtype, down = {"e4m3": (ml_dtypes.float8_e4m3fn, 7), "e5m2": (ml_dtypes.float8_e5m2, 14)}[fmt]
    v = np.moveaxis(np.asarray(x, np.float32).astype(ml_dtypes.bfloat16).astype(np.float64), axis, -1)
    blocks = v.reshape(v.shape[:-1] + (-1, 32))
    amax = np.abs(blocks).max(-1, keepdims=True)
    byte = np.maximum(np.where(amax > 0, np.frexp(amax)[1] - 1 + 127, 0) - down, 1)
    scale = np.exp2(byte - 127.0)
    codes = (blocks / scale).astype(np.float32).astype(dtype).astype(np.float64)
    return np.moveaxis((codes * scale).reshape(v.shape), -1, axis)


WIDE = False


def mx_kscale(k):
    if not WIDE:
        return np.ones(k)
    levels = np.array([10, -10, 5, -5, 0])
    a = np.random.permutation(np.resize(levels, k // 512 * 4)).reshape(k // 512, 4)
    idx = np.arange(k)
    return np.exp2(a[idx // 512, idx % 128 // 32])


BF16 = ml_dtypes.bfloat16


def bf(x):
    return np.asarray(x, np.float32).astype(BF16)


def f64(x):
    return np.asarray(x).astype(np.float64)


N, T1, U, T2 = 512, 512, 128, 512
W_BASE = 6


def setup_inputs():
    s1, s2 = mx_kscale(T1), mx_kscale(T2)
    g = 0.8 / N ** 0.25
    return {
        "x1": bf(np.random.standard_normal((N, T1)) * s1),
        "x2": bf(np.random.standard_normal((N, T2)) * s2),
        "w1": bf(np.random.standard_normal((U, T1)) * g / np.sqrt(T1) / s1),
        "b1": bf(np.random.standard_normal(U) * 0.5 / np.sqrt(N)),
        "w2": bf(np.random.standard_normal((T2, T2)) * g / np.sqrt(T2) / s2),
        "b2": bf(np.random.standard_normal(T2) * 0.5 / np.sqrt(N)),
        "global_att": bf(np.random.standard_normal((T2, U))),
        "i": 2,
        "j": 3,
    }


def reference(x1, x2, w1, b1, w2, b2, global_att, i, j):
    n2 = x2.shape[1]
    wind = W_BASE + int(i)
    r = wind // 2 - 1
    x1p = ((mxq(f64(x1), 1, "e4m3") @ mxq(f64(w1), 1, "e4m3").T) + f64(b1)).T
    x2p = (mxq(f64(x2), 1, "e4m3") @ mxq(f64(w2), 1, "e4m3").T) + f64(b2)
    ti = mxq(x1p, 1, "e4m3") @ mxq(x2p, 0, "e4m3")
    used = (n2 // wind) * wind
    tip = np.pad(ti, ((0, 0), (r, r)))
    out = sum(tip[:, d:d + used] for d in range(2 * r + 1))
    if used < n2:
        out = np.pad(out, ((0, 0), (n2 - used, 0)))
    local_att = out.T
    lg = local_att + f64(global_att)
    e = np.exp(lg - lg.max(axis=0, keepdims=True))
    return e / e.sum(axis=0, keepdims=True)

@@ -1,0 +1,240 @@
+import concourse.masks as masks
+import concourse.mybir as mybir
+
+F32 = mybir.dt.float32
+BF16 = mybir.dt.bfloat16
+U32 = mybir.dt.uint32
+U8 = mybir.dt.uint8
+FP8X4 = mybir.dt.float8_e4m3fn_x4
+ADD = mybir.AluOpType.add
+MAX = mybir.AluOpType.max
+EXP = mybir.ActivationFunctionType.Exp
+ALONG_FREE = mybir.AxisListType.X
+
+P = 128
+PACK = 4
+ROWS = 512
+T = 512
+U = 128
+K = 512
+ROW_TILES = ROWS // P
+K_TILES = K // P
+HALF_WINDOW = 3
+
+FLOPS = 2 * (ROWS * T * U + ROWS * T * K + U * ROWS * K)
+
+
+def quantise_rows(nc, psum, identity, rows, grouped, codes, scales):
+    tiles = rows.shape[1]
+    words = rows.bitcast(F32)
+    flipped = psum.tile([P, tiles, 2, P], F32, tag="bank")
+    for i in range(tiles):
+        for h in range(2):
+            nc.tensor.transpose(flipped[:, i, h, :], words[:, i, h * P : (h + 1) * P], identity)
+    nc.scalar.copy(out=grouped.bitcast(F32), in_=flipped[:].rearrange("q i h r -> q i r h"))
+    nc.vector.quantize_mx(
+        out=codes.bitcast(FP8X4),
+        scales=scales,
+        in_=grouped.rearrange("q i r v -> q (i r v)"),
+    )
+
+
+def tile_swd_s_kernel(tc, x1, x2, w1, b1, w2, b2, global_att, i, j, out):
+    nc = tc.nc
+    assert (6 + i) // 2 - 1 == HALF_WINDOW and K % (6 + i) == 0
+
+    with tc.tile_pool(name="keep", bufs=1) as keep, tc.psum_pool(
+        name="psum", bufs=8
+    ) as psum, tc.manual_schedule():
+        x1_sb = keep.tile([P, ROW_TILES, T], BF16)
+        x2_sb = keep.tile([P, ROW_TILES, T], BF16)
+        w1_sb = keep.tile([P, 1, T], BF16)
+        w2_sb = keep.tile([P, K_TILES, T], BF16)
+        ga_sb = keep.tile([P, PACK, U], BF16)
+        x1_rows = x1.rearrange("(p j) t -> p j t", j=ROW_TILES)
+        x2_rows = x2.rearrange("(p j) t -> p j t", j=ROW_TILES)
+        w2_rows = w2.rearrange("(m p) t -> p m t", p=P)
+        nc.sync.dma_start(out=x1_sb[:, 0:2, :], in_=x1_rows[:, 0:2, :])
+        nc.sync.dma_start(out=x1_sb[:, 2:4, :], in_=x1_rows[:, 2:4, :])
+        nc.sync.dma_start(out=w1_sb[:, 0, :], in_=w1)
+        nc.sync.dma_start(out=x2_sb[:, 0:2, :], in_=x2_rows[:, 0:2, :])
+        nc.sync.dma_start(out=x2_sb[:, 2:4, :], in_=x2_rows[:, 2:4, :])
+        nc.sync.dma_start(out=w2_sb[:, 0:2, :], in_=w2_rows[:, 0:2, :])
+        nc.sync.dma_start(out=w2_sb[:, 2:4, :], in_=w2_rows[:, 2:4, :])
+        nc.sync.dma_start(out=ga_sb[:], in_=global_att.rearrange("(p m) u -> p m u", m=PACK))
+
+        bias_rows = keep.tile([P, K + U], BF16)
+        nc.vector.memset(bias_rows[:], 0.0)
+        nc.scalar.dma_start(out=bias_rows[0:1, 0:K], in_=b2.rearrange("(o k) -> o k", o=1))
+        nc.scalar.dma_start(out=bias_rows[0:1, K : K + U], in_=b1.rearrange("(o u) -> o u", o=1))
+        ones = keep.tile([P, P], BF16)
+        nc.vector.memset(ones[:], 1.0)
+        exp_in = keep.tile([P, 1], F32)
+        exp_out = keep.tile([P, 1], F32)
+        nc.vector.memset(exp_in[:], 0.0)
+        nc.scalar.activation(out=exp_out[:], in_=exp_in[:], func=EXP)
+        ti_pad = keep.tile([P, K + 2 * HALF_WINDOW], F32)
+        nc.vector.memset(ti_pad[:], 0.0)
+        ident_f32 = keep.tile([P, P], F32)
+        masks.make_identity(nc, ident_f32[:])
+        ident_bf16 = keep.tile([P, P], BF16)
+        nc.vector.tensor_copy(out=ident_bf16[:], in_=ident_f32[:])
+
+        b2_bank = psum.tile([P, K], F32, tag="bank")
+        b1_bank = psum.tile([P, U], F32, tag="bank")
+        nc.tensor.matmul(out=b1_bank[:], lhsT=ones[:], rhs=bias_rows[:, K : K + U], start=True, stop=True)
+        nc.tensor.matmul(out=b2_bank[:], lhsT=ones[:], rhs=bias_rows[:, 0:K], start=True, stop=True)
+        b1_all = keep.tile([P, U], F32)
+        b2_all = keep.tile([P, K], F32)
+        nc.vector.tensor_copy(out=b1_all[:], in_=b1_bank[:])
+        nc.vector.tensor_copy(out=b2_all[:], in_=b2_bank[:])
+
+        x1_grouped = keep.tile([P, ROW_TILES, P, PACK], BF16, align_bytes=64)
+        x2_grouped = keep.tile([P, ROW_TILES, P, PACK], BF16, align_bytes=64)
+        w1_grouped = keep.tile([P, 1, P, PACK], BF16, align_bytes=64)
+        w2_grouped = keep.tile([P, K_TILES, P, PACK], BF16, align_bytes=64)
+        a_grouped = keep.tile([P, U, PACK], BF16, align_bytes=64)
+        c_grouped = keep.tile([P, K_TILES, P, PACK], BF16, align_bytes=64)
+        x1_codes = keep.tile([P, ROWS], U32, align_bytes=64)
+        x2_codes = keep.tile([P, ROWS], U32, align_bytes=64)
+        w1_codes = keep.tile([P, U], U32, align_bytes=64)
+        w2_codes = keep.tile([P, K], U32, align_bytes=64)
+        a_codes = keep.tile([P, U], U32, align_bytes=64)
+        c_codes = keep.tile([P, K], U32, align_bytes=64)
+        x1_scales = keep.tile([P, ROWS], U8, align_bytes=64)
+        x2_scales = keep.tile([P, ROWS], U8, align_bytes=64)
+        w1_scales = keep.tile([P, U], U8, align_bytes=64)
+        w2_scales = keep.tile([P, K], U8, align_bytes=64)
+        a_scales = keep.tile([P, U], U8, align_bytes=64)
+        c_scales = keep.tile([P, K], U8, align_bytes=64)
+
+        def quantise_pair(rows_sb, grouped, codes, scales, pair):
+            tiles = slice(2 * pair, 2 * pair + 2)
+            cols = slice(2 * pair * P, (2 * pair + 2) * P)
+            quantise_rows(
+                nc, psum, ident_f32[:], rows_sb[:, tiles, :], grouped[:, tiles, :, :],
+                codes[:, cols], scales[:, cols],
+            )
+
+        quantise_pair(x1_sb, x1_grouped, x1_codes, x1_scales, 0)
+        quantise_pair(x1_sb, x1_grouped, x1_codes, x1_scales, 1)
+        quantise_rows(nc, psum, ident_f32[:], w1_sb[:], w1_grouped[:], w1_codes[:], w1_scales[:])
+        quantise_pair(x2_sb, x2_grouped, x2_codes, x2_scales, 0)
+
+        a_bank = psum.tile([P, ROW_TILES, U], F32, tag="bank")
+        for jj in range(ROW_TILES):
+            tile_cols = slice(jj * P, (jj + 1) * P)
+            nc.tensor.matmul_mx(
+                out=a_bank[:, jj, :],
+                lhsT=x1_codes[:, tile_cols].bitcast(FP8X4),
+                lhsT_scale=x1_scales[:, tile_cols],
+                rhs=w1_codes[:].bitcast(FP8X4),
+                rhs_scale=w1_scales[:],
+                start=True,
+                stop=True,
+            )
+        nc.vector.tensor_tensor(
+            out=a_grouped[:],
+            in0=a_bank[:].rearrange("p j u -> p u j"),
+            in1=b1_all[:].unsqueeze(2).to_broadcast([P, U, PACK]),
+            op=ADD,
+        )
+        quantise_pair(x2_sb, x2_grouped, x2_codes, x2_scales, 1)
+        nc.vector.quantize_mx(
+            out=a_codes[:].bitcast(FP8X4),
+            scales=a_scales[:],
+            in_=a_grouped[:].rearrange("p u j -> p (u j)"),
+        )
+        quantise_pair(w2_sb, w2_grouped, w2_codes, w2_scales, 0)
+        quantise_pair(w2_sb, w2_grouped, w2_codes, w2_scales, 1)
+
+        ga_flipped = psum.tile([P, PACK, P], BF16, tag="bank")
+        for m in range(PACK):
+            nc.tensor.transpose(ga_flipped[:, m, :], ga_sb[:, m, :], ident_bf16[:])
+        ga_t = keep.tile([P, P, PACK], F32)
+        nc.scalar.copy(out=ga_t[:], in_=ga_flipped[:].rearrange("u m p -> u p m"))
+
+        def quantise_c(m):
+            cols = slice(m * P, (m + 1) * P)
+            nc.vector.quantize_mx(
+                out=c_codes[:, cols].bitcast(FP8X4),
+                scales=c_scales[:, cols],
+                in_=c_grouped[:, m, :, :].rearrange("p k j -> p (k j)"),
+            )
+
+        for m in range(K_TILES):
+            k_cols = slice(m * P, (m + 1) * P)
+            c_bank = psum.tile([P, ROW_TILES, P], F32, tag="bank")
+            for jj in range(ROW_TILES):
+                tile_cols = slice(jj * P, (jj + 1) * P)
+                nc.tensor.matmul_mx(
+                    out=c_bank[:, jj, :],
+                    lhsT=x2_codes[:, tile_cols].bitcast(FP8X4),
+                    lhsT_scale=x2_scales[:, tile_cols],
+                    rhs=w2_codes[:, k_cols].bitcast(FP8X4),
+                    rhs_scale=w2_scales[:, k_cols],
+                    start=True,
+                    stop=True,
+                )
+            nc.vector.tensor_tensor(
+                out=c_grouped[:, m, :, :],
+                in0=c_bank[:].rearrange("p j k -> p k j"),
+                in1=b2_all[:, k_cols].unsqueeze(2).to_broadcast([P, P, PACK]),
+                op=ADD,
+            )
+            if m >= 1:
+                quantise_c(m - 1)
+        quantise_c(K_TILES - 1)
+
+        ti_bank = psum.tile([P, K], F32, tag="bank")
+        nc.tensor.matmul_mx(
+            out=ti_bank[:],
+            lhsT=a_codes[:].bitcast(FP8X4),
+            lhsT_scale=a_scales[:],
+            rhs=c_codes[:].bitcast(FP8X4),
+            rhs_scale=c_scales[:],
+            start=True,
+            stop=True,
+        )
+        nc.scalar.copy(out=ti_pad[:, HALF_WINDOW : HALF_WINDOW + K], in_=ti_bank[:])
+
+        sum2 = keep.tile([P, K + 4], F32)
+        last_ga = keep.tile([P, K], F32)
+        sum4 = keep.tile([P, K], F32)
+        rest = keep.tile([P, K], F32)
+        logits = keep.tile([P, K], F32)
+        nc.vector.tensor_tensor(out=sum2[:], in0=ti_pad[:, 0 : K + 4], in1=ti_pad[:, 1 : K + 5], op=ADD)
+        nc.vector.tensor_tensor(
+            out=last_ga[:], in0=ti_pad[:, 6 : K + 6], in1=ga_t[:].rearrange("u p m -> u (p m)"), op=ADD
+        )
+        nc.vector.tensor_tensor(out=sum4[:], in0=sum2[:, 0:K], in1=sum2[:, 2 : K + 2], op=ADD)
+        nc.vector.tensor_tensor(out=rest[:], in0=sum2[:, 4 : K + 4], in1=last_ga[:], op=ADD)
+        nc.vector.tensor_tensor(out=logits[:], in0=sum4[:], in1=rest[:], op=ADD)
+
+        neg_max = keep.tile([P, 1], F32)
+        exp_sum = keep.tile([P, 1], F32)
+        inv_sum = keep.tile([P, 1], F32)
+        expd = keep.tile([P, K], F32)
+        prob = keep.tile([P, K], F32)
+        nc.vector.tensor_reduce(out=neg_max[:], in_=logits[:], axis=ALONG_FREE, op=MAX, negate=True)
+        nc.scalar.activation(
+            out=expd[:], in_=logits[:], func=EXP, bias=neg_max[:, 0:1], scale=1.0, accum_out=exp_sum[:, 0:1]
+        )
+        nc.vector.reciprocal(out=inv_sum[:], in_=exp_sum[:])
+
+        out_sb = keep.tile([P, K_TILES, U], F32)
+        out_rows = out.rearrange("(m p) u -> p m u", p=P)
+        for half in range(2):
+            cols = slice(half * 2 * P, (half + 1) * 2 * P)
+            nc.vector.tensor_scalar_mul(out=prob[:, cols], in0=expd[:, cols], scalar1=inv_sum[:, 0:1])
+        for half in range(2):
+            tiles = slice(2 * half, 2 * half + 2)
+            out_bank = psum.tile([P, 2, U], F32, tag="bank")
+            for i2 in range(2):
+                m = 2 * half + i2
+                nc.tensor.transpose(out_bank[:, i2, :], prob[:, m * P : (m + 1) * P], ident_f32[:])
+            if half == 0:
+                nc.vector.tensor_copy(out=out_sb[:, tiles, :], in_=out_bank[:])
+            else:
+                nc.scalar.copy(out=out_sb[:, tiles, :], in_=out_bank[:])
+            nc.sync.dma_start(out=out_rows[:, tiles, :], in_=out_sb[:, tiles, :])

@@ -8,6 +8,7 @@ U8 = mybir.dt.uint8
 FP8X4 = mybir.dt.float8_e4m3fn_x4
 ADD = mybir.AluOpType.add
 MAX = mybir.AluOpType.max
+IS_GE = mybir.AluOpType.is_ge
 EXP = mybir.ActivationFunctionType.Exp
 ALONG_FREE = mybir.AxisListType.X
 
@@ -19,7 +20,10 @@ U = 128
 K = 512
 ROW_TILES = ROWS // P
 K_TILES = K // P
-HALF_WINDOW = 3
+
+WINDOW_STEP = 64
+WINDOWS = (K - P) // WINDOW_STEP + 1
+EDGE = (P - WINDOW_STEP) // 2
 
 FLOPS = 2 * (ROWS * T * U + ROWS * T * K + U * ROWS * K)
 
@@ -27,7 +31,7 @@ FLOPS = 2 * (ROWS * T * U + ROWS * T * K + U * ROWS * K)
 def quantise_rows(nc, psum, identity, rows, grouped, codes, scales):
     tiles = rows.shape[1]
     words = rows.bitcast(F32)
-    flipped = psum.tile([P, tiles, 2, P], F32, tag="bank")
+    flipped = psum.tile([P, tiles, 2, P], F32, tag="work")
     for i in range(tiles):
         for h in range(2):
             nc.tensor.transpose(flipped[:, i, h, :], words[:, i, h * P : (h + 1) * P], identity)
@@ -41,10 +45,11 @@ def quantise_rows(nc, psum, identity, rows, grouped, codes, scales):
 
 def tile_swd_s_kernel(tc, x1, x2, w1, b1, w2, b2, global_att, i, j, out):
     nc = tc.nc
-    assert (6 + i) // 2 - 1 == HALF_WINDOW and K % (6 + i) == 0
+    half_window = (6 + i) // 2 - 1
+    assert K % (6 + i) == 0 and half_window <= EDGE
 
     with tc.tile_pool(name="keep", bufs=1) as keep, tc.psum_pool(
-        name="psum", bufs=8
+        name="psum", bufs=7
     ) as psum, tc.manual_schedule():
         x1_sb = keep.tile([P, ROW_TILES, T], BF16)
         x2_sb = keep.tile([P, ROW_TILES, T], BF16)
@@ -53,35 +58,42 @@ def tile_swd_s_kernel(tc, x1, x2, w1, b1, w2, b2, global_att, i, j, out):
         ga_sb = keep.tile([P, PACK, U], BF16)
         x1_rows = x1.rearrange("(p j) t -> p j t", j=ROW_TILES)
         x2_rows = x2.rearrange("(p j) t -> p j t", j=ROW_TILES)
-        w2_rows = w2.rearrange("(m p) t -> p m t", p=P)
         nc.sync.dma_start(out=x1_sb[:, 0:2, :], in_=x1_rows[:, 0:2, :])
         nc.sync.dma_start(out=x1_sb[:, 2:4, :], in_=x1_rows[:, 2:4, :])
         nc.sync.dma_start(out=w1_sb[:, 0, :], in_=w1)
         nc.sync.dma_start(out=x2_sb[:, 0:2, :], in_=x2_rows[:, 0:2, :])
         nc.sync.dma_start(out=x2_sb[:, 2:4, :], in_=x2_rows[:, 2:4, :])
-        nc.sync.dma_start(out=w2_sb[:, 0:2, :], in_=w2_rows[:, 0:2, :])
-        nc.sync.dma_start(out=w2_sb[:, 2:4, :], in_=w2_rows[:, 2:4, :])
+        for m in range(K_TILES):
+            nc.sync.dma_start(out=w2_sb[:, m, :], in_=w2[m * P : (m + 1) * P, :])
         nc.sync.dma_start(out=ga_sb[:], in_=global_att.rearrange("(p m) u -> p m u", m=PACK))
 
         bias_rows = keep.tile([P, K + U], BF16)
-        nc.vector.memset(bias_rows[:], 0.0)
-        nc.scalar.dma_start(out=bias_rows[0:1, 0:K], in_=b2.rearrange("(o k) -> o k", o=1))
-        nc.scalar.dma_start(out=bias_rows[0:1, K : K + U], in_=b1.rearrange("(o u) -> o u", o=1))
+        nc.scalar.dma_start(out=bias_rows[P - 1 : P, K : K + U], in_=b1.rearrange("(o u) -> o u", o=1))
+        nc.scalar.dma_start(out=bias_rows[P - 1 : P, 0:K], in_=b2.rearrange("(o k) -> o k", o=1))
+        nc.vector.memset(bias_rows[0 : P - 1, :], 0.0)
         ones = keep.tile([P, P], BF16)
         nc.vector.memset(ones[:], 1.0)
         exp_in = keep.tile([P, 1], F32)
         exp_out = keep.tile([P, 1], F32)
         nc.vector.memset(exp_in[:], 0.0)
         nc.scalar.activation(out=exp_out[:], in_=exp_in[:], func=EXP)
-        ti_pad = keep.tile([P, K + 2 * HALF_WINDOW], F32)
-        nc.vector.memset(ti_pad[:], 0.0)
         ident_f32 = keep.tile([P, P], F32)
         masks.make_identity(nc, ident_f32[:])
         ident_bf16 = keep.tile([P, P], BF16)
         nc.vector.tensor_copy(out=ident_bf16[:], in_=ident_f32[:])
+        band = keep.tile([P, P], F32)
+        nc.gpsimd.memset(band[:], 1.0)
+        nc.gpsimd.affine_select(
+            out=band[:], in_=band[:], pattern=[[-1, P]], compare_op=IS_GE, fill=0.0,
+            base=half_window, channel_multiplier=1,
+        )
+        nc.gpsimd.affine_select(
+            out=band[:], in_=band[:], pattern=[[1, P]], compare_op=IS_GE, fill=0.0,
+            base=half_window, channel_multiplier=-1,
+        )
 
-        b2_bank = psum.tile([P, K], F32, tag="bank")
-        b1_bank = psum.tile([P, U], F32, tag="bank")
+        b1_bank = psum.tile([P, U], F32, tag="work")
+        b2_bank = psum.tile([P, K], F32, tag="work")
         nc.tensor.matmul(out=b1_bank[:], lhsT=ones[:], rhs=bias_rows[:, K : K + U], start=True, stop=True)
         nc.tensor.matmul(out=b2_bank[:], lhsT=ones[:], rhs=bias_rows[:, 0:K], start=True, stop=True)
         b1_all = keep.tile([P, U], F32)
@@ -108,114 +120,113 @@ def tile_swd_s_kernel(tc, x1, x2, w1, b1, w2, b2, global_att, i, j, out):
         a_scales = keep.tile([P, U], U8, align_bytes=64)
         c_scales = keep.tile([P, K], U8, align_bytes=64)
 
-        def quantise_pair(rows_sb, grouped, codes, scales, pair):
-            tiles = slice(2 * pair, 2 * pair + 2)
-            cols = slice(2 * pair * P, (2 * pair + 2) * P)
+        def quantise_tiles(rows_sb, grouped, codes, scales, first, count):
+            tiles = slice(first, first + count)
+            cols = slice(first * P, (first + count) * P)
             quantise_rows(
                 nc, psum, ident_f32[:], rows_sb[:, tiles, :], grouped[:, tiles, :, :],
                 codes[:, cols], scales[:, cols],
             )
 
-        quantise_pair(x1_sb, x1_grouped, x1_codes, x1_scales, 0)
-        quantise_pair(x1_sb, x1_grouped, x1_codes, x1_scales, 1)
-        quantise_rows(nc, psum, ident_f32[:], w1_sb[:], w1_grouped[:], w1_codes[:], w1_scales[:])
-        quantise_pair(x2_sb, x2_grouped, x2_codes, x2_scales, 0)
+        def product_bank(x_codes, x_scales, w_codes, w_scales):
+            bank = psum.tile([P, ROW_TILES, P], F32, tag="work")
+            for jj in range(ROW_TILES):
+                tile_cols = slice(jj * P, (jj + 1) * P)
+                nc.tensor.matmul_mx(
+                    out=bank[:, jj, :],
+                    lhsT=x_codes[:, tile_cols].bitcast(FP8X4),
+                    lhsT_scale=x_scales[:, tile_cols],
+                    rhs=w_codes.bitcast(FP8X4),
+                    rhs_scale=w_scales,
+                    start=True,
+                    stop=True,
+                )
+            return bank
 
-        a_bank = psum.tile([P, ROW_TILES, U], F32, tag="bank")
-        for jj in range(ROW_TILES):
-            tile_cols = slice(jj * P, (jj + 1) * P)
-            nc.tensor.matmul_mx(
-                out=a_bank[:, jj, :],
-                lhsT=x1_codes[:, tile_cols].bitcast(FP8X4),
-                lhsT_scale=x1_scales[:, tile_cols],
-                rhs=w1_codes[:].bitcast(FP8X4),
-                rhs_scale=w1_scales[:],
-                start=True,
-                stop=True,
+        def add_bias(bank, bias, grouped):
+            nc.vector.tensor_tensor(
+                out=grouped,
+                in0=bank[:].rearrange("p j s -> p s j"),
+                in1=bias.unsqueeze(2).to_broadcast([P, P, PACK]),
+                op=ADD,
             )
-        nc.vector.tensor_tensor(
-            out=a_grouped[:],
-            in0=a_bank[:].rearrange("p j u -> p u j"),
-            in1=b1_all[:].unsqueeze(2).to_broadcast([P, U, PACK]),
-            op=ADD,
-        )
-        quantise_pair(x2_sb, x2_grouped, x2_codes, x2_scales, 1)
-        nc.vector.quantize_mx(
-            out=a_codes[:].bitcast(FP8X4),
-            scales=a_scales[:],
-            in_=a_grouped[:].rearrange("p u j -> p (u j)"),
-        )
-        quantise_pair(w2_sb, w2_grouped, w2_codes, w2_scales, 0)
-        quantise_pair(w2_sb, w2_grouped, w2_codes, w2_scales, 1)
 
-        ga_flipped = psum.tile([P, PACK, P], BF16, tag="bank")
+        def quantise_columns(grouped, codes, scales):
+            nc.vector.quantize_mx(
+                out=codes.bitcast(FP8X4), scales=scales, in_=grouped.rearrange("p s j -> p (s j)")
+            )
+
+        quantise_tiles(x1_sb, x1_grouped, x1_codes, x1_scales, 0, 2)
+        quantise_tiles(x1_sb, x1_grouped, x1_codes, x1_scales, 2, 2)
+        quantise_tiles(w1_sb, w1_grouped, w1_codes, w1_scales, 0, 1)
+        quantise_tiles(x2_sb, x2_grouped, x2_codes, x2_scales, 0, 2)
+        quantise_tiles(x2_sb, x2_grouped, x2_codes, x2_scales, 2, 2)
+        a_bank = product_bank(x1_codes, x1_scales, w1_codes[:], w1_scales[:])
+        add_bias(a_bank, b1_all[:], a_grouped[:])
+        quantise_tiles(w2_sb, w2_grouped, w2_codes, w2_scales, 0, 1)
+        quantise_columns(a_grouped[:], a_codes[:], a_scales[:])
+        for m in range(1, K_TILES):
+            quantise_tiles(w2_sb, w2_grouped, w2_codes, w2_scales, m, 1)
+
+        c_banks = []
+        for m in range(K_TILES):
+            k_cols = slice(m * P, (m + 1) * P)
+            c_banks.append(product_bank(x2_codes, x2_scales, w2_codes[:, k_cols], w2_scales[:, k_cols]))
+
+        ga_flipped = psum.tile([P, PACK, P], BF16, tag="work")
         for m in range(PACK):
             nc.tensor.transpose(ga_flipped[:, m, :], ga_sb[:, m, :], ident_bf16[:])
         ga_t = keep.tile([P, P, PACK], F32)
         nc.scalar.copy(out=ga_t[:], in_=ga_flipped[:].rearrange("u m p -> u p m"))
 
-        def quantise_c(m):
-            cols = slice(m * P, (m + 1) * P)
-            nc.vector.quantize_mx(
-                out=c_codes[:, cols].bitcast(FP8X4),
-                scales=c_scales[:, cols],
-                in_=c_grouped[:, m, :, :].rearrange("p k j -> p (k j)"),
-            )
+        ti_t = keep.tile([P, WINDOWS, U], F32)
+        loc_bank = psum.tile([P, K], F32, tag="loc", bufs=1)
 
-        for m in range(K_TILES):
-            k_cols = slice(m * P, (m + 1) * P)
-            c_bank = psum.tile([P, ROW_TILES, P], F32, tag="bank")
-            for jj in range(ROW_TILES):
-                tile_cols = slice(jj * P, (jj + 1) * P)
-                nc.tensor.matmul_mx(
-                    out=c_bank[:, jj, :],
-                    lhsT=x2_codes[:, tile_cols].bitcast(FP8X4),
-                    lhsT_scale=x2_scales[:, tile_cols],
-                    rhs=w2_codes[:, k_cols].bitcast(FP8X4),
-                    rhs_scale=w2_scales[:, k_cols],
-                    start=True,
-                    stop=True,
-                )
-            nc.vector.tensor_tensor(
-                out=c_grouped[:, m, :, :],
-                in0=c_bank[:].rearrange("p j k -> p k j"),
-                in1=b2_all[:, k_cols].unsqueeze(2).to_broadcast([P, P, PACK]),
-                op=ADD,
-            )
-            if m >= 1:
-                quantise_c(m - 1)
-        quantise_c(K_TILES - 1)
+        def windows_ending_in(m):
+            return [w for w in range(WINDOWS) if (w * WINDOW_STEP + P - 1) // P == m]
 
-        ti_bank = psum.tile([P, K], F32, tag="bank")
-        nc.tensor.matmul_mx(
-            out=ti_bank[:],
-            lhsT=a_codes[:].bitcast(FP8X4),
-            lhsT_scale=a_scales[:],
-            rhs=c_codes[:].bitcast(FP8X4),
-            rhs_scale=c_scales[:],
-            start=True,
-            stop=True,
-        )
-        nc.scalar.copy(out=ti_pad[:, HALF_WINDOW : HALF_WINDOW + K], in_=ti_bank[:])
+        for step in range(K_TILES + 2):
+            if step < K_TILES:
+                add_bias(c_banks[step], b2_all[:, step * P : (step + 1) * P], c_grouped[:, step, :, :])
+            if 1 <= step <= K_TILES:
+                m = step - 1
+                k_cols = slice(m * P, (m + 1) * P)
+                quantise_columns(c_grouped[:, m, :, :], c_codes[:, k_cols], c_scales[:, k_cols])
+                ready = windows_ending_in(m)
+                ti_t_bank = psum.tile([P, len(ready), U], F32, tag="work")
+                for place, w in enumerate(ready):
+                    window = slice(w * WINDOW_STEP, w * WINDOW_STEP + P)
+                    nc.tensor.matmul_mx(
+                        out=ti_t_bank[:, place, :],
+                        lhsT=c_codes[:, window].bitcast(FP8X4),
+                        lhsT_scale=c_scales[:, window],
+                        rhs=a_codes[:].bitcast(FP8X4),
+                        rhs_scale=a_scales[:],
+                        start=True,
+                        stop=True,
+                    )
+                nc.scalar.copy(out=ti_t[:, ready[0] : ready[0] + len(ready), :], in_=ti_t_bank[:])
+            if step >= 2:
+                for w in windows_ending_in(step - 2):
+                    first = 0 if w == 0 else EDGE
+                    last = P if w == WINDOWS - 1 else P - EDGE
+                    nc.tensor.matmul(
+                        out=loc_bank[:, w * WINDOW_STEP + first : w * WINDOW_STEP + last],
+                        lhsT=ti_t[:, w, :],
+                        rhs=band[:, first:last],
+                        start=True,
+                        stop=True,
+                    )
 
-        sum2 = keep.tile([P, K + 4], F32)
-        last_ga = keep.tile([P, K], F32)
-        sum4 = keep.tile([P, K], F32)
-        rest = keep.tile([P, K], F32)
         logits = keep.tile([P, K], F32)
-        nc.vector.tensor_tensor(out=sum2[:], in0=ti_pad[:, 0 : K + 4], in1=ti_pad[:, 1 : K + 5], op=ADD)
-        nc.vector.tensor_tensor(
-            out=last_ga[:], in0=ti_pad[:, 6 : K + 6], in1=ga_t[:].rearrange("u p m -> u (p m)"), op=ADD
-        )
-        nc.vector.tensor_tensor(out=sum4[:], in0=sum2[:, 0:K], in1=sum2[:, 2 : K + 2], op=ADD)
-        nc.vector.tensor_tensor(out=rest[:], in0=sum2[:, 4 : K + 4], in1=last_ga[:], op=ADD)
-        nc.vector.tensor_tensor(out=logits[:], in0=sum4[:], in1=rest[:], op=ADD)
-
         neg_max = keep.tile([P, 1], F32)
         exp_sum = keep.tile([P, 1], F32)
         inv_sum = keep.tile([P, 1], F32)
         expd = keep.tile([P, K], F32)
         prob = keep.tile([P, K], F32)
+        nc.vector.tensor_tensor(
+            out=logits[:], in0=loc_bank[:], in1=ga_t[:].rearrange("u p m -> u (p m)"), op=ADD
+        )
         nc.vector.tensor_reduce(out=neg_max[:], in_=logits[:], axis=ALONG_FREE, op=MAX, negate=True)
         nc.scalar.activation(
             out=expd[:], in_=logits[:], func=EXP, bias=neg_max[:, 0:1], scale=1.0, accum_out=exp_sum[:, 0:1]
@@ -229,10 +240,10 @@ def tile_swd_s_kernel(tc, x1, x2, w1, b1, w2, b2, global_att, i, j, out):
             nc.vector.tensor_scalar_mul(out=prob[:, cols], in0=expd[:, cols], scalar1=inv_sum[:, 0:1])
         for half in range(2):
             tiles = slice(2 * half, 2 * half + 2)
-            out_bank = psum.tile([P, 2, U], F32, tag="bank")
-            for i2 in range(2):
-                m = 2 * half + i2
-                nc.tensor.transpose(out_bank[:, i2, :], prob[:, m * P : (m + 1) * P], ident_f32[:])
+            out_bank = psum.tile([P, 2, U], F32, tag="work")
+            for place in range(2):
+                m = 2 * half + place
+                nc.tensor.transpose(out_bank[:, place, :], prob[:, m * P : (m + 1) * P], ident_f32[:])
             if half == 0:
                 nc.vector.tensor_copy(out=out_sb[:, tiles, :], in_=out_bank[:])
             else:

@@ -10,6 +10,7 @@ ADD = mybir.AluOpType.add
 MAX = mybir.AluOpType.max
 IS_GE = mybir.AluOpType.is_ge
 EXP = mybir.ActivationFunctionType.Exp
+COPY = mybir.ActivationFunctionType.Copy
 ALONG_FREE = mybir.AxisListType.X
 
 P = 128
@@ -20,10 +21,6 @@ U = 128
 K = 512
 ROW_TILES = ROWS // P
 K_TILES = K // P
-
-WINDOW_STEP = 64
-WINDOWS = (K - P) // WINDOW_STEP + 1
-EDGE = (P - WINDOW_STEP) // 2
 
 FLOPS = 2 * (ROWS * T * U + ROWS * T * K + U * ROWS * K)
 
@@ -46,7 +43,7 @@ def quantise_rows(nc, psum, identity, rows, grouped, codes, scales):
 def tile_swd_s_kernel(tc, x1, x2, w1, b1, w2, b2, global_att, i, j, out):
     nc = tc.nc
     half_window = (6 + i) // 2 - 1
-    assert K % (6 + i) == 0 and half_window <= EDGE
+    assert K % (6 + i) == 0
 
     with tc.tile_pool(name="keep", bufs=1) as keep, tc.psum_pool(
         name="psum", bufs=7
@@ -55,17 +52,18 @@ def tile_swd_s_kernel(tc, x1, x2, w1, b1, w2, b2, global_att, i, j, out):
         x2_sb = keep.tile([P, ROW_TILES, T], BF16)
         w1_sb = keep.tile([P, 1, T], BF16)
         w2_sb = keep.tile([P, K_TILES, T], BF16)
-        ga_sb = keep.tile([P, PACK, U], BF16)
+        ga_sb = keep.tile([P, K_TILES, U], BF16)
         x1_rows = x1.rearrange("(p j) t -> p j t", j=ROW_TILES)
         x2_rows = x2.rearrange("(p j) t -> p j t", j=ROW_TILES)
-        nc.sync.dma_start(out=x1_sb[:, 0:2, :], in_=x1_rows[:, 0:2, :])
+        nc.sync.dma_start(out=x1_sb[:, 0, :], in_=x1_rows[:, 0, :])
+        nc.sync.dma_start(out=x1_sb[:, 1, :], in_=x1_rows[:, 1, :])
         nc.sync.dma_start(out=x1_sb[:, 2:4, :], in_=x1_rows[:, 2:4, :])
         nc.sync.dma_start(out=w1_sb[:, 0, :], in_=w1)
         nc.sync.dma_start(out=x2_sb[:, 0:2, :], in_=x2_rows[:, 0:2, :])
         nc.sync.dma_start(out=x2_sb[:, 2:4, :], in_=x2_rows[:, 2:4, :])
         for m in range(K_TILES):
             nc.sync.dma_start(out=w2_sb[:, m, :], in_=w2[m * P : (m + 1) * P, :])
-        nc.sync.dma_start(out=ga_sb[:], in_=global_att.rearrange("(p m) u -> p m u", m=PACK))
+        nc.sync.dma_start(out=ga_sb[:], in_=global_att.rearrange("(m p) u -> p m u", p=P))
 
         bias_rows = keep.tile([P, K + U], BF16)
         nc.scalar.dma_start(out=bias_rows[P - 1 : P, K : K + U], in_=b1.rearrange("(o u) -> o u", o=1))
@@ -79,17 +77,16 @@ def tile_swd_s_kernel(tc, x1, x2, w1, b1, w2, b2, global_att, i, j, out):
         nc.scalar.activation(out=exp_out[:], in_=exp_in[:], func=EXP)
         ident_f32 = keep.tile([P, P], F32)
         masks.make_identity(nc, ident_f32[:])
-        ident_bf16 = keep.tile([P, P], BF16)
-        nc.vector.tensor_copy(out=ident_bf16[:], in_=ident_f32[:])
-        band = keep.tile([P, P], F32)
+        band_cols = P + 2 * half_window
+        band = keep.tile([P, band_cols], F32)
         nc.gpsimd.memset(band[:], 1.0)
         nc.gpsimd.affine_select(
-            out=band[:], in_=band[:], pattern=[[-1, P]], compare_op=IS_GE, fill=0.0,
-            base=half_window, channel_multiplier=1,
+            out=band[:], in_=band[:], pattern=[[1, band_cols]], compare_op=IS_GE, fill=0.0,
+            base=0, channel_multiplier=-1,
         )
         nc.gpsimd.affine_select(
-            out=band[:], in_=band[:], pattern=[[1, P]], compare_op=IS_GE, fill=0.0,
-            base=half_window, channel_multiplier=-1,
+            out=band[:], in_=band[:], pattern=[[-1, band_cols]], compare_op=IS_GE, fill=0.0,
+            base=2 * half_window, channel_multiplier=1,
         )
 
         b1_bank = psum.tile([P, U], F32, tag="work")
@@ -173,18 +170,20 @@ def tile_swd_s_kernel(tc, x1, x2, w1, b1, w2, b2, global_att, i, j, out):
             k_cols = slice(m * P, (m + 1) * P)
             c_banks.append(product_bank(x2_codes, x2_scales, w2_codes[:, k_cols], w2_scales[:, k_cols]))
 
-        ga_flipped = psum.tile([P, PACK, P], BF16, tag="work")
-        for m in range(PACK):
-            nc.tensor.transpose(ga_flipped[:, m, :], ga_sb[:, m, :], ident_bf16[:])
-        ga_t = keep.tile([P, P, PACK], F32)
-        nc.scalar.copy(out=ga_t[:], in_=ga_flipped[:].rearrange("u m p -> u p m"))
+        ga_f32 = keep.tile([P, K_TILES, U], F32)
+        nc.scalar.copy(out=ga_f32[:], in_=ga_sb[:])
+        logits_bank = psum.tile([P, K], F32, tag="logits", bufs=1)
+        for m in range(K_TILES):
+            nc.tensor.matmul(
+                out=logits_bank[:, m * P : (m + 1) * P],
+                lhsT=ga_f32[:, m, :],
+                rhs=ident_f32[:],
+                is_transpose=True,
+                start=(m == 0),
+                stop=False,
+            )
 
-        ti_t = keep.tile([P, WINDOWS, U], F32)
-        loc_bank = psum.tile([P, K], F32, tag="loc", bufs=1)
-
-        def windows_ending_in(m):
-            return [w for w in range(WINDOWS) if (w * WINDOW_STEP + P - 1) // P == m]
-
+        ti_t = keep.tile([P, K_TILES, U], F32)
         for step in range(K_TILES + 2):
             if step < K_TILES:
                 add_bias(c_banks[step], b2_all[:, step * P : (step + 1) * P], c_grouped[:, step, :, :])
@@ -192,52 +191,46 @@ def tile_swd_s_kernel(tc, x1, x2, w1, b1, w2, b2, global_att, i, j, out):
                 m = step - 1
                 k_cols = slice(m * P, (m + 1) * P)
                 quantise_columns(c_grouped[:, m, :, :], c_codes[:, k_cols], c_scales[:, k_cols])
-                ready = windows_ending_in(m)
-                ti_t_bank = psum.tile([P, len(ready), U], F32, tag="work")
-                for place, w in enumerate(ready):
-                    window = slice(w * WINDOW_STEP, w * WINDOW_STEP + P)
-                    nc.tensor.matmul_mx(
-                        out=ti_t_bank[:, place, :],
-                        lhsT=c_codes[:, window].bitcast(FP8X4),
-                        lhsT_scale=c_scales[:, window],
-                        rhs=a_codes[:].bitcast(FP8X4),
-                        rhs_scale=a_scales[:],
-                        start=True,
-                        stop=True,
-                    )
-                nc.scalar.copy(out=ti_t[:, ready[0] : ready[0] + len(ready), :], in_=ti_t_bank[:])
+                ti_t_bank = psum.tile([P, U], F32, tag="work")
+                nc.tensor.matmul_mx(
+                    out=ti_t_bank[:],
+                    lhsT=c_codes[:, k_cols].bitcast(FP8X4),
+                    lhsT_scale=c_scales[:, k_cols],
+                    rhs=a_codes[:].bitcast(FP8X4),
+                    rhs_scale=a_scales[:],
+                    start=True,
+                    stop=True,
+                )
+                nc.scalar.copy(out=ti_t[:, m, :], in_=ti_t_bank[:])
             if step >= 2:
-                for w in windows_ending_in(step - 2):
-                    first = 0 if w == 0 else EDGE
-                    last = P if w == WINDOWS - 1 else P - EDGE
-                    nc.tensor.matmul(
-                        out=loc_bank[:, w * WINDOW_STEP + first : w * WINDOW_STEP + last],
-                        lhsT=ti_t[:, w, :],
-                        rhs=band[:, first:last],
-                        start=True,
-                        stop=True,
-                    )
+                m = step - 2
+                origin = m * P - half_window
+                low = max(origin, 0)
+                high = min(origin + band_cols, K)
+                nc.tensor.matmul(
+                    out=logits_bank[:, low:high],
+                    lhsT=ti_t[:, m, :],
+                    rhs=band[:, low - origin : high - origin],
+                    start=False,
+                    stop=(m == K_TILES - 1),
+                )
 
-        logits = keep.tile([P, K], F32)
         neg_max = keep.tile([P, 1], F32)
         exp_sum = keep.tile([P, 1], F32)
         inv_sum = keep.tile([P, 1], F32)
         expd = keep.tile([P, K], F32)
         prob = keep.tile([P, K], F32)
-        nc.vector.tensor_tensor(
-            out=logits[:], in0=loc_bank[:], in1=ga_t[:].rearrange("u p m -> u (p m)"), op=ADD
-        )
-        nc.vector.tensor_reduce(out=neg_max[:], in_=logits[:], axis=ALONG_FREE, op=MAX, negate=True)
+        nc.vector.tensor_reduce(out=neg_max[:], in_=logits_bank[:], axis=ALONG_FREE, op=MAX, negate=True)
         nc.scalar.activation(
-            out=expd[:], in_=logits[:], func=EXP, bias=neg_max[:, 0:1], scale=1.0, accum_out=exp_sum[:, 0:1]
+            out=expd[:], in_=logits_bank[:], func=EXP, bias=neg_max[:, 0:1], scale=1.0,
+            accum_out=exp_sum[:, 0:1],
         )
         nc.vector.reciprocal(out=inv_sum[:], in_=exp_sum[:])
 
         out_sb = keep.tile([P, K_TILES, U], F32)
         out_rows = out.rearrange("(m p) u -> p m u", p=P)
-        for half in range(2):
-            cols = slice(half * 2 * P, (half + 1) * 2 * P)
-            nc.vector.tensor_scalar_mul(out=prob[:, cols], in0=expd[:, cols], scalar1=inv_sum[:, 0:1])
+        nc.vector.tensor_scalar_mul(out=prob[:, 0 : K // 2], in0=expd[:, 0 : K // 2], scalar1=inv_sum[:, 0:1])
+        nc.scalar.activation(out=prob[:, K // 2 : K], in_=expd[:, K // 2 : K], func=COPY, scale=inv_sum[:, 0:1])
         for half in range(2):
             tiles = slice(2 * half, 2 * half + 2)
             out_bank = psum.tile([P, 2, U], F32, tag="work")

@@ -7,11 +7,11 @@ U32 = mybir.dt.uint32
 U8 = mybir.dt.uint8
 FP8X4 = mybir.dt.float8_e4m3fn_x4
 ADD = mybir.AluOpType.add
-MAX = mybir.AluOpType.max
+MIN = mybir.AluOpType.min
+MULT = mybir.AluOpType.mult
 IS_GE = mybir.AluOpType.is_ge
 EXP = mybir.ActivationFunctionType.Exp
 COPY = mybir.ActivationFunctionType.Copy
-ALONG_FREE = mybir.AxisListType.X
 
 P = 128
 PACK = 4
@@ -21,6 +21,7 @@ U = 128
 K = 512
 ROW_TILES = ROWS // P
 K_TILES = K // P
+IDLE_PASSES = 5
 
 FLOPS = 2 * (ROWS * T * U + ROWS * T * K + U * ROWS * K)
 
@@ -46,7 +47,7 @@ def tile_swd_s_kernel(tc, x1, x2, w1, b1, w2, b2, global_att, i, j, out):
     assert K % (6 + i) == 0
 
     with tc.tile_pool(name="keep", bufs=1) as keep, tc.psum_pool(
-        name="psum", bufs=7
+        name="psum", bufs=6
     ) as psum, tc.manual_schedule():
         x1_sb = keep.tile([P, ROW_TILES, T], BF16)
         x2_sb = keep.tile([P, ROW_TILES, T], BF16)
@@ -77,16 +78,17 @@ def tile_swd_s_kernel(tc, x1, x2, w1, b1, w2, b2, global_att, i, j, out):
         nc.scalar.activation(out=exp_out[:], in_=exp_in[:], func=EXP)
         ident_f32 = keep.tile([P, P], F32)
         masks.make_identity(nc, ident_f32[:])
-        band_cols = P + 2 * half_window
+        reach = half_window + 1
+        band_cols = P + 2 * reach
         band = keep.tile([P, band_cols], F32)
         nc.gpsimd.memset(band[:], 1.0)
         nc.gpsimd.affine_select(
             out=band[:], in_=band[:], pattern=[[1, band_cols]], compare_op=IS_GE, fill=0.0,
-            base=0, channel_multiplier=-1,
+            base=half_window - reach, channel_multiplier=-1,
         )
         nc.gpsimd.affine_select(
             out=band[:], in_=band[:], pattern=[[-1, band_cols]], compare_op=IS_GE, fill=0.0,
-            base=2 * half_window, channel_multiplier=1,
+            base=reach + half_window, channel_multiplier=1,
         )
 
         b1_bank = psum.tile([P, U], F32, tag="work")
@@ -170,18 +172,41 @@ def tile_swd_s_kernel(tc, x1, x2, w1, b1, w2, b2, global_att, i, j, out):
             k_cols = slice(m * P, (m + 1) * P)
             c_banks.append(product_bank(x2_codes, x2_scales, w2_codes[:, k_cols], w2_scales[:, k_cols]))
 
+        early_cols = (K_TILES - 1) * P - reach
+        late_origin = (K_TILES - 2) * P
         ga_f32 = keep.tile([P, K_TILES, U], F32)
         nc.scalar.copy(out=ga_f32[:], in_=ga_sb[:])
-        logits_bank = psum.tile([P, K], F32, tag="logits", bufs=1)
-        for m in range(K_TILES):
+        early_bank = psum.tile([P, (K_TILES - 1) * P], F32, tag="early", bufs=1)
+        late_bank = psum.tile([P, 2 * P], F32, tag="late", bufs=1)
+
+        def lay_global_att(bank, origin, m, first):
             nc.tensor.matmul(
-                out=logits_bank[:, m * P : (m + 1) * P],
+                out=bank[:, m * P - origin : (m + 1) * P - origin],
                 lhsT=ga_f32[:, m, :],
                 rhs=ident_f32[:],
                 is_transpose=True,
-                start=(m == 0),
+                start=first,
                 stop=False,
             )
+
+        for m in range(K_TILES - 1):
+            lay_global_att(early_bank, 0, m, m == 0)
+        for m in range(K_TILES - 2, K_TILES):
+            lay_global_att(late_bank, late_origin, m, m == K_TILES - 2)
+
+        def spread(bank, origin, m, low, high, last):
+            window = m * P - reach
+            nc.tensor.matmul(
+                out=bank[:, low - origin : high - origin],
+                lhsT=ti_t[:, m, :],
+                rhs=band[:, low - window : high - window],
+                start=False,
+                stop=last,
+            )
+
+        neg_logits = keep.tile([P, K], F32)
+        neg_max_early = keep.tile([P, 1], F32)
+        neg_max = keep.tile([P, 1], F32)
 
         ti_t = keep.tile([P, K_TILES, U], F32)
         for step in range(K_TILES + 2):
@@ -204,41 +229,56 @@ def tile_swd_s_kernel(tc, x1, x2, w1, b1, w2, b2, global_att, i, j, out):
                 nc.scalar.copy(out=ti_t[:, m, :], in_=ti_t_bank[:])
             if step >= 2:
                 m = step - 2
-                origin = m * P - half_window
-                low = max(origin, 0)
-                high = min(origin + band_cols, K)
-                nc.tensor.matmul(
-                    out=logits_bank[:, low:high],
-                    lhsT=ti_t[:, m, :],
-                    rhs=band[:, low - origin : high - origin],
-                    start=False,
-                    stop=(m == K_TILES - 1),
-                )
+                low = max(m * P - reach, 0)
+                high = min((m + 1) * P + reach, K)
+                if low < early_cols:
+                    spread(early_bank, 0, m, low, min(high, early_cols), high > early_cols)
+                if high > early_cols:
+                    spread(late_bank, late_origin, m, max(low, early_cols), high, m == K_TILES - 1)
+                if low < early_cols < high:
+                    nc.vector.tensor_scalar(
+                        out=neg_logits[:, 0:early_cols], in0=early_bank[:, 0:early_cols], scalar1=-1.0,
+                        scalar2=None, op0=MULT, op1=MIN, accum_out=neg_max_early[:, 0:1],
+                    )
 
-        neg_max = keep.tile([P, 1], F32)
+        for i in range(IDLE_PASSES):
+            idle_bank = psum.tile([P, K], F32, tag="work")
+            nc.tensor.matmul_mx(
+                out=idle_bank[:],
+                lhsT=c_codes[:, 0:P].bitcast(FP8X4),
+                lhsT_scale=c_scales[:, 0:P],
+                rhs=c_codes[:].bitcast(FP8X4),
+                rhs_scale=c_scales[:],
+                start=True,
+                stop=True,
+            )
+
         exp_sum = keep.tile([P, 1], F32)
         inv_sum = keep.tile([P, 1], F32)
         expd = keep.tile([P, K], F32)
         prob = keep.tile([P, K], F32)
-        nc.vector.tensor_reduce(out=neg_max[:], in_=logits_bank[:], axis=ALONG_FREE, op=MAX, negate=True)
+        nc.vector.tensor_scalar(
+            out=neg_logits[:, early_cols:K], in0=late_bank[:, early_cols - late_origin : K - late_origin],
+            scalar1=-1.0, scalar2=neg_max_early[:, 0:1], op0=MULT, op1=MIN, accum_out=neg_max[:, 0:1],
+        )
         nc.scalar.activation(
-            out=expd[:], in_=logits_bank[:], func=EXP, bias=neg_max[:, 0:1], scale=1.0,
+            out=expd[:], in_=neg_logits[:], func=EXP, bias=neg_max[:, 0:1], scale=-1.0,
             accum_out=exp_sum[:, 0:1],
         )
         nc.vector.reciprocal(out=inv_sum[:], in_=exp_sum[:])
 
         out_sb = keep.tile([P, K_TILES, U], F32)
         out_rows = out.rearrange("(m p) u -> p m u", p=P)
-        nc.vector.tensor_scalar_mul(out=prob[:, 0 : K // 2], in0=expd[:, 0 : K // 2], scalar1=inv_sum[:, 0:1])
-        nc.scalar.activation(out=prob[:, K // 2 : K], in_=expd[:, K // 2 : K], func=COPY, scale=inv_sum[:, 0:1])
+        nc.vector.tensor_scalar_mul(out=prob[:, 0:P], in0=expd[:, 0:P], scalar1=inv_sum[:, 0:1])
+        nc.scalar.activation(out=prob[:, 3 * P : K], in_=expd[:, 3 * P : K], func=COPY, scale=inv_sum[:, 0:1])
+        nc.vector.tensor_scalar_mul(out=prob[:, P : 3 * P], in0=expd[:, P : 3 * P], scalar1=inv_sum[:, 0:1])
+        for m in range(K_TILES):
+            out_bank = psum.tile([P, U], F32, tag="work")
+            nc.tensor.transpose(out_bank[:], prob[:, m * P : (m + 1) * P], ident_f32[:])
+            if m % 2 == 0:
+                nc.vector.tensor_copy(out=out_sb[:, m, :], in_=out_bank[:])
+            else:
+                nc.scalar.copy(out=out_sb[:, m, :], in_=out_bank[:])
         for half in range(2):
             tiles = slice(2 * half, 2 * half + 2)
-            out_bank = psum.tile([P, 2, U], F32, tag="work")
-            for place in range(2):
-                m = 2 * half + place
-                nc.tensor.transpose(out_bank[:, place, :], prob[:, m * P : (m + 1) * P], ident_f32[:])
-            if half == 0:
-                nc.vector.tensor_copy(out=out_sb[:, tiles, :], in_=out_bank[:])
-            else:
-                nc.scalar.copy(out=out_sb[:, tiles, :], in_=out_bank[:])
             nc.sync.dma_start(out=out_rows[:, tiles, :], in_=out_sb[:, tiles, :])

@@ -26,21 +26,6 @@ IDLE_PASSES = 5
 FLOPS = 2 * (ROWS * T * U + ROWS * T * K + U * ROWS * K)
 
 
-def quantise_rows(nc, psum, identity, rows, grouped, codes, scales):
-    tiles = rows.shape[1]
-    words = rows.bitcast(F32)
-    flipped = psum.tile([P, tiles, 2, P], F32, tag="work")
-    for i in range(tiles):
-        for h in range(2):
-            nc.tensor.transpose(flipped[:, i, h, :], words[:, i, h * P : (h + 1) * P], identity)
-    nc.scalar.copy(out=grouped.bitcast(F32), in_=flipped[:].rearrange("q i h r -> q i r h"))
-    nc.vector.quantize_mx(
-        out=codes.bitcast(FP8X4),
-        scales=scales,
-        in_=grouped.rearrange("q i r v -> q (i r v)"),
-    )
-
-
 def tile_swd_s_kernel(tc, x1, x2, w1, b1, w2, b2, global_att, i, j, out):
     nc = tc.nc
     half_window = (6 + i) // 2 - 1
@@ -119,12 +104,23 @@ def tile_swd_s_kernel(tc, x1, x2, w1, b1, w2, b2, global_att, i, j, out):
         a_scales = keep.tile([P, U], U8, align_bytes=64)
         c_scales = keep.tile([P, K], U8, align_bytes=64)
 
-        def quantise_tiles(rows_sb, grouped, codes, scales, first, count):
-            tiles = slice(first, first + count)
+        def flip(rows_sb, grouped, first, count):
+            words = rows_sb[:, first : first + count, :].bitcast(F32)
+            flipped = psum.tile([P, count, 2, P], F32, tag="work")
+            for i in range(count):
+                for h in range(2):
+                    nc.tensor.transpose(flipped[:, i, h, :], words[:, i, h * P : (h + 1) * P], ident_f32[:])
+            nc.scalar.copy(
+                out=grouped[:, first : first + count, :, :].bitcast(F32),
+                in_=flipped[:].rearrange("q i h r -> q i r h"),
+            )
+
+        def quantise(grouped, codes, scales, first, count):
             cols = slice(first * P, (first + count) * P)
-            quantise_rows(
-                nc, psum, ident_f32[:], rows_sb[:, tiles, :], grouped[:, tiles, :, :],
-                codes[:, cols], scales[:, cols],
+            nc.vector.quantize_mx(
+                out=codes[:, cols].bitcast(FP8X4),
+                scales=scales[:, cols],
+                in_=grouped[:, first : first + count, :, :].rearrange("q i r v -> q (i r v)"),
             )
 
         def product_bank(x_codes, x_scales, w_codes, w_scales):
@@ -150,27 +146,53 @@ def tile_swd_s_kernel(tc, x1, x2, w1, b1, w2, b2, global_att, i, j, out):
                 op=ADD,
             )
 
-        def quantise_columns(grouped, codes, scales):
+        def c_product(m):
+            k_cols = slice(m * P, (m + 1) * P)
+            return product_bank(x2_codes, x2_scales, w2_codes[:, k_cols], w2_scales[:, k_cols])
+
+        def c_bias(m, bank):
+            add_bias(bank, b2_all[:, m * P : (m + 1) * P], c_grouped[:, m, :, :])
+
+        def quantise_c(m):
+            quantise(c_grouped, c_codes, c_scales, m, 1)
+
+        def quantise_a():
             nc.vector.quantize_mx(
-                out=codes.bitcast(FP8X4), scales=scales, in_=grouped.rearrange("p s j -> p (s j)")
+                out=a_codes[:].bitcast(FP8X4), scales=a_scales[:], in_=a_grouped[:].rearrange("p s j -> p (s j)")
             )
 
-        quantise_tiles(x1_sb, x1_grouped, x1_codes, x1_scales, 0, 2)
-        quantise_tiles(x1_sb, x1_grouped, x1_codes, x1_scales, 2, 2)
-        quantise_tiles(w1_sb, w1_grouped, w1_codes, w1_scales, 0, 1)
-        quantise_tiles(x2_sb, x2_grouped, x2_codes, x2_scales, 0, 2)
-        quantise_tiles(x2_sb, x2_grouped, x2_codes, x2_scales, 2, 2)
+        flip(x1_sb, x1_grouped, 0, 1)
+        flip(x1_sb, x1_grouped, 1, 1)
+        quantise(x1_grouped, x1_codes, x1_scales, 0, 1)
+        flip(x1_sb, x1_grouped, 2, 2)
+        quantise(x1_grouped, x1_codes, x1_scales, 1, 1)
+        flip(w1_sb, w1_grouped, 0, 1)
+        quantise(x1_grouped, x1_codes, x1_scales, 2, 2)
+        flip(x2_sb, x2_grouped, 0, 2)
+        quantise(w1_grouped, w1_codes, w1_scales, 0, 1)
+        flip(x2_sb, x2_grouped, 2, 2)
+        quantise(x2_grouped, x2_codes, x2_scales, 0, 2)
+        flip(w2_sb, w2_grouped, 0, 1)
+        quantise(x2_grouped, x2_codes, x2_scales, 2, 2)
+        flip(w2_sb, w2_grouped, 1, 1)
         a_bank = product_bank(x1_codes, x1_scales, w1_codes[:], w1_scales[:])
+        quantise(w2_grouped, w2_codes, w2_scales, 0, 1)
+        flip(w2_sb, w2_grouped, 2, 1)
         add_bias(a_bank, b1_all[:], a_grouped[:])
-        quantise_tiles(w2_sb, w2_grouped, w2_codes, w2_scales, 0, 1)
-        quantise_columns(a_grouped[:], a_codes[:], a_scales[:])
-        for m in range(1, K_TILES):
-            quantise_tiles(w2_sb, w2_grouped, w2_codes, w2_scales, m, 1)
-
-        c_banks = []
-        for m in range(K_TILES):
-            k_cols = slice(m * P, (m + 1) * P)
-            c_banks.append(product_bank(x2_codes, x2_scales, w2_codes[:, k_cols], w2_scales[:, k_cols]))
+        flip(w2_sb, w2_grouped, 3, 1)
+        quantise(w2_grouped, w2_codes, w2_scales, 1, 1)
+        quantise(w2_grouped, w2_codes, w2_scales, 2, 1)
+        quantise_a()
+        quantise(w2_grouped, w2_codes, w2_scales, 3, 1)
+        c_banks = [c_product(m) for m in range(K_TILES)]
+        c_bias(0, c_banks[0])
+        c_bias(1, c_banks[1])
+        quantise_c(0)
+        c_bias(2, c_banks[2])
+        quantise_c(1)
+        c_bias(3, c_banks[3])
+        quantise_c(2)
+        quantise_c(3)
 
         early_cols = (K_TILES - 1) * P - reach
         late_origin = (K_TILES - 2) * P
@@ -189,6 +211,23 @@ def tile_swd_s_kernel(tc, x1, x2, w1, b1, w2, b2, global_att, i, j, out):
                 stop=False,
             )
 
+        ti_t = keep.tile([P, K_TILES, U], F32)
+
+        def ti_product(m):
+            k_cols = slice(m * P, (m + 1) * P)
+            ti_t_bank = psum.tile([P, U], F32, tag="work")
+            nc.tensor.matmul_mx(
+                out=ti_t_bank[:],
+                lhsT=c_codes[:, k_cols].bitcast(FP8X4),
+                lhsT_scale=c_scales[:, k_cols],
+                rhs=a_codes[:].bitcast(FP8X4),
+                rhs_scale=a_scales[:],
+                start=True,
+                stop=True,
+            )
+            nc.scalar.copy(out=ti_t[:, m, :], in_=ti_t_bank[:])
+
+        ti_product(0)
         for m in range(K_TILES - 1):
             lay_global_att(early_bank, 0, m, m == 0)
         for m in range(K_TILES - 2, K_TILES):
@@ -208,38 +247,25 @@ def tile_swd_s_kernel(tc, x1, x2, w1, b1, w2, b2, global_att, i, j, out):
         neg_max_early = keep.tile([P, 1], F32)
         neg_max = keep.tile([P, 1], F32)
 
-        ti_t = keep.tile([P, K_TILES, U], F32)
-        for step in range(K_TILES + 2):
-            if step < K_TILES:
-                add_bias(c_banks[step], b2_all[:, step * P : (step + 1) * P], c_grouped[:, step, :, :])
-            if 1 <= step <= K_TILES:
-                m = step - 1
-                k_cols = slice(m * P, (m + 1) * P)
-                quantise_columns(c_grouped[:, m, :, :], c_codes[:, k_cols], c_scales[:, k_cols])
-                ti_t_bank = psum.tile([P, U], F32, tag="work")
-                nc.tensor.matmul_mx(
-                    out=ti_t_bank[:],
-                    lhsT=c_codes[:, k_cols].bitcast(FP8X4),
-                    lhsT_scale=c_scales[:, k_cols],
-                    rhs=a_codes[:].bitcast(FP8X4),
-                    rhs_scale=a_scales[:],
-                    start=True,
-                    stop=True,
-                )
-                nc.scalar.copy(out=ti_t[:, m, :], in_=ti_t_bank[:])
-            if step >= 2:
-                m = step - 2
-                low = max(m * P - reach, 0)
-                high = min((m + 1) * P + reach, K)
-                if low < early_cols:
-                    spread(early_bank, 0, m, low, min(high, early_cols), high > early_cols)
-                if high > early_cols:
-                    spread(late_bank, late_origin, m, max(low, early_cols), high, m == K_TILES - 1)
-                if low < early_cols < high:
-                    nc.vector.tensor_scalar(
-                        out=neg_logits[:, 0:early_cols], in0=early_bank[:, 0:early_cols], scalar1=-1.0,
-                        scalar2=None, op0=MULT, op1=MIN, accum_out=neg_max_early[:, 0:1],
-                    )
+        def spread_tile(m):
+            low = max(m * P - reach, 0)
+            high = min((m + 1) * P + reach, K)
+            if low < early_cols:
+                spread(early_bank, 0, m, low, min(high, early_cols), high > early_cols)
+            if high > early_cols:
+                spread(late_bank, late_origin, m, max(low, early_cols), high, m == K_TILES - 1)
+
+        ti_product(1)
+        spread_tile(0)
+        ti_product(2)
+        ti_product(3)
+        spread_tile(1)
+        spread_tile(2)
+        nc.vector.tensor_scalar(
+            out=neg_logits[:, 0:early_cols], in0=early_bank[:, 0:early_cols], scalar1=-1.0,
+            scalar2=None, op0=MULT, op1=MIN, accum_out=neg_max_early[:, 0:1],
+        )
+        spread_tile(3)
 
         for i in range(IDLE_PASSES):
             idle_bank = psum.tile([P, K], F32, tag="work")

@@ -22,6 +22,7 @@ K = 512
 ROW_TILES = ROWS // P
 K_TILES = K // P
 IDLE_PASSES = 5
+EARLY_TILES = 2
 
 FLOPS = 2 * (ROWS * T * U + ROWS * T * K + U * ROWS * K)
 
@@ -194,12 +195,12 @@ def tile_swd_s_kernel(tc, x1, x2, w1, b1, w2, b2, global_att, i, j, out):
         quantise_c(2)
         quantise_c(3)
 
-        early_cols = (K_TILES - 1) * P - reach
-        late_origin = (K_TILES - 2) * P
+        early_cols = EARLY_TILES * P - reach
+        late_origin = (EARLY_TILES - 1) * P
         ga_f32 = keep.tile([P, K_TILES, U], F32)
         nc.scalar.copy(out=ga_f32[:], in_=ga_sb[:])
-        early_bank = psum.tile([P, (K_TILES - 1) * P], F32, tag="early", bufs=1)
-        late_bank = psum.tile([P, 2 * P], F32, tag="late", bufs=1)
+        early_bank = psum.tile([P, EARLY_TILES * P], F32, tag="early", bufs=1)
+        late_bank = psum.tile([P, K - late_origin], F32, tag="late", bufs=1)
 
         def lay_global_att(bank, origin, m, first):
             nc.tensor.matmul(
@@ -228,10 +229,10 @@ def tile_swd_s_kernel(tc, x1, x2, w1, b1, w2, b2, global_att, i, j, out):
             nc.scalar.copy(out=ti_t[:, m, :], in_=ti_t_bank[:])
 
         ti_product(0)
-        for m in range(K_TILES - 1):
+        for m in range(EARLY_TILES):
             lay_global_att(early_bank, 0, m, m == 0)
-        for m in range(K_TILES - 2, K_TILES):
-            lay_global_att(late_bank, late_origin, m, m == K_TILES - 2)
+        for m in range(EARLY_TILES - 1, K_TILES):
+            lay_global_att(late_bank, late_origin, m, m == EARLY_TILES - 1)
 
         def spread(bank, origin, m, low, high, last):
             window = m * P - reach
@@ -260,11 +261,11 @@ def tile_swd_s_kernel(tc, x1, x2, w1, b1, w2, b2, global_att, i, j, out):
         ti_product(2)
         ti_product(3)
         spread_tile(1)
-        spread_tile(2)
         nc.vector.tensor_scalar(
             out=neg_logits[:, 0:early_cols], in0=early_bank[:, 0:early_cols], scalar1=-1.0,
             scalar2=None, op0=MULT, op1=MIN, accum_out=neg_max_early[:, 0:1],
         )
+        spread_tile(2)
         spread_tile(3)
 
         for i in range(IDLE_PASSES):

@@ -22,6 +22,7 @@ K = 512
 ROW_TILES = ROWS // P
 K_TILES = K // P
 IDLE_PASSES = 5
+WARM_UP_PASSES = 12
 EARLY_TILES = 2
 
 FLOPS = 2 * (ROWS * T * U + ROWS * T * K + U * ROWS * K)
@@ -55,9 +56,14 @@ def tile_swd_s_kernel(tc, x1, x2, w1, b1, w2, b2, global_att, i, j, out):
         bias_rows = keep.tile([P, K + U], BF16)
         nc.scalar.dma_start(out=bias_rows[P - 1 : P, K : K + U], in_=b1.rearrange("(o u) -> o u", o=1))
         nc.scalar.dma_start(out=bias_rows[P - 1 : P, 0:K], in_=b2.rearrange("(o k) -> o k", o=1))
-        nc.vector.memset(bias_rows[0 : P - 1, :], 0.0)
         ones = keep.tile([P, P], BF16)
+        zeros = keep.tile([P, P * PACK], BF16, align_bytes=64)
+        zero_codes = keep.tile([P, P], U32, align_bytes=64)
+        zero_scales = keep.tile([P, P], U8, align_bytes=64)
+        nc.vector.memset(zeros[:].bitcast(U32), 0)
         nc.vector.memset(ones[:], 1.0)
+        nc.vector.quantize_mx(out=zero_codes[:].bitcast(FP8X4), scales=zero_scales[:], in_=zeros[:])
+        nc.vector.memset(bias_rows[0 : P - 1, :].bitcast(U32), 0)
         exp_in = keep.tile([P, 1], F32)
         exp_out = keep.tile([P, 1], F32)
         nc.vector.memset(exp_in[:], 0.0)
@@ -77,6 +83,17 @@ def tile_swd_s_kernel(tc, x1, x2, w1, b1, w2, b2, global_att, i, j, out):
             base=reach + half_window, channel_multiplier=1,
         )
 
+        warm_bank = psum.tile([P, P], F32, tag="work")
+        for i in range(WARM_UP_PASSES):
+            nc.tensor.matmul_mx(
+                out=warm_bank[:],
+                lhsT=zero_codes[:].bitcast(FP8X4),
+                lhsT_scale=zero_scales[:],
+                rhs=zero_codes[:].bitcast(FP8X4),
+                rhs_scale=zero_scales[:],
+                start=True,
+                stop=True,
+            )
         b1_bank = psum.tile([P, U], F32, tag="work")
         b2_bank = psum.tile([P, K], F32, tag="work")
         nc.tensor.matmul(out=b1_bank[:], lhsT=ones[:], rhs=bias_rows[:, K : K + U], start=True, stop=True)
@@ -105,16 +122,12 @@ def tile_swd_s_kernel(tc, x1, x2, w1, b1, w2, b2, global_att, i, j, out):
         a_scales = keep.tile([P, U], U8, align_bytes=64)
         c_scales = keep.tile([P, K], U8, align_bytes=64)
 
-        def flip(rows_sb, grouped, first, count):
-            words = rows_sb[:, first : first + count, :].bitcast(F32)
-            flipped = psum.tile([P, count, 2, P], F32, tag="work")
-            for i in range(count):
-                for h in range(2):
-                    nc.tensor.transpose(flipped[:, i, h, :], words[:, i, h * P : (h + 1) * P], ident_f32[:])
-            nc.scalar.copy(
-                out=grouped[:, first : first + count, :, :].bitcast(F32),
-                in_=flipped[:].rearrange("q i h r -> q i r h"),
-            )
+        def flip(rows_sb, grouped, i, copy):
+            words = rows_sb[:, i, :].bitcast(F32)
+            flipped = psum.tile([P, 2, P], F32, tag="work")
+            for h in range(2):
+                nc.tensor.transpose(flipped[:, h, :], words[:, h * P : (h + 1) * P], ident_f32[:])
+            copy(out=grouped[:, i, :, :].bitcast(F32), in_=flipped[:].rearrange("q h r -> q r h"))
 
         def quantise(grouped, codes, scales, first, count):
             cols = slice(first * P, (first + count) * P)
@@ -162,28 +175,35 @@ def tile_swd_s_kernel(tc, x1, x2, w1, b1, w2, b2, global_att, i, j, out):
                 out=a_codes[:].bitcast(FP8X4), scales=a_scales[:], in_=a_grouped[:].rearrange("p s j -> p (s j)")
             )
 
-        flip(x1_sb, x1_grouped, 0, 1)
-        flip(x1_sb, x1_grouped, 1, 1)
+        on_scalar, on_vector = nc.scalar.copy, nc.vector.tensor_copy
+        flip(x1_sb, x1_grouped, 0, on_scalar)
+        flip(x1_sb, x1_grouped, 1, on_scalar)
         quantise(x1_grouped, x1_codes, x1_scales, 0, 1)
-        flip(x1_sb, x1_grouped, 2, 2)
+        flip(x1_sb, x1_grouped, 2, on_scalar)
         quantise(x1_grouped, x1_codes, x1_scales, 1, 1)
-        flip(w1_sb, w1_grouped, 0, 1)
-        quantise(x1_grouped, x1_codes, x1_scales, 2, 2)
-        flip(x2_sb, x2_grouped, 0, 2)
+        flip(x1_sb, x1_grouped, 3, on_vector)
+        flip(w1_sb, w1_grouped, 0, on_scalar)
+        quantise(x1_grouped, x1_codes, x1_scales, 2, 1)
+        flip(x2_sb, x2_grouped, 0, on_scalar)
+        quantise(x1_grouped, x1_codes, x1_scales, 3, 1)
+        flip(x2_sb, x2_grouped, 1, on_scalar)
         quantise(w1_grouped, w1_codes, w1_scales, 0, 1)
-        flip(x2_sb, x2_grouped, 2, 2)
-        quantise(x2_grouped, x2_codes, x2_scales, 0, 2)
-        flip(w2_sb, w2_grouped, 0, 1)
-        quantise(x2_grouped, x2_codes, x2_scales, 2, 2)
-        flip(w2_sb, w2_grouped, 1, 1)
+        flip(x2_sb, x2_grouped, 2, on_scalar)
+        quantise(x2_grouped, x2_codes, x2_scales, 0, 1)
+        flip(x2_sb, x2_grouped, 3, on_scalar)
+        quantise(x2_grouped, x2_codes, x2_scales, 1, 1)
+        flip(w2_sb, w2_grouped, 0, on_scalar)
+        quantise(x2_grouped, x2_codes, x2_scales, 2, 1)
         a_bank = product_bank(x1_codes, x1_scales, w1_codes[:], w1_scales[:])
+        quantise(x2_grouped, x2_codes, x2_scales, 3, 1)
+        flip(w2_sb, w2_grouped, 1, on_scalar)
         quantise(w2_grouped, w2_codes, w2_scales, 0, 1)
-        flip(w2_sb, w2_grouped, 2, 1)
+        flip(w2_sb, w2_grouped, 2, on_scalar)
         add_bias(a_bank, b1_all[:], a_grouped[:])
-        flip(w2_sb, w2_grouped, 3, 1)
+        flip(w2_sb, w2_grouped, 3, on_scalar)
         quantise(w2_grouped, w2_codes, w2_scales, 1, 1)
-        quantise(w2_grouped, w2_codes, w2_scales, 2, 1)
         quantise_a()
+        quantise(w2_grouped, w2_codes, w2_scales, 2, 1)
         quantise(w2_grouped, w2_codes, w2_scales, 3, 1)
         c_banks = [c_product(m) for m in range(K_TILES)]
         c_bias(0, c_banks[0])

@@ -194,16 +194,16 @@ def tile_swd_s_kernel(tc, x1, x2, w1, b1, w2, b2, global_att, i, j, out):
         quantise(x2_grouped, x2_codes, x2_scales, 1, 1)
         flip(w2_sb, w2_grouped, 0, on_scalar)
         quantise(x2_grouped, x2_codes, x2_scales, 2, 1)
-        a_bank = product_bank(x1_codes, x1_scales, w1_codes[:], w1_scales[:])
-        quantise(x2_grouped, x2_codes, x2_scales, 3, 1)
         flip(w2_sb, w2_grouped, 1, on_scalar)
+        quantise(x2_grouped, x2_codes, x2_scales, 3, 1)
+        a_bank = product_bank(x1_codes, x1_scales, w1_codes[:], w1_scales[:])
         quantise(w2_grouped, w2_codes, w2_scales, 0, 1)
         flip(w2_sb, w2_grouped, 2, on_scalar)
         add_bias(a_bank, b1_all[:], a_grouped[:])
         flip(w2_sb, w2_grouped, 3, on_scalar)
         quantise(w2_grouped, w2_codes, w2_scales, 1, 1)
-        quantise_a()
         quantise(w2_grouped, w2_codes, w2_scales, 2, 1)
+        quantise_a()
         quantise(w2_grouped, w2_codes, w2_scales, 3, 1)
         c_banks = [c_product(m) for m in range(K_TILES)]
         c_bias(0, c_banks[0])

@@ -21,7 +21,7 @@ U = 128
 K = 512
 ROW_TILES = ROWS // P
 K_TILES = K // P
-IDLE_PASSES = 5
+IDLE_PASSES = 3
 WARM_UP_PASSES = 12
 EARLY_TILES = 2
 

import concourse.masks as masks
import concourse.mybir as mybir

F32 = mybir.dt.float32
BF16 = mybir.dt.bfloat16
U32 = mybir.dt.uint32
U8 = mybir.dt.uint8
FP8X4 = mybir.dt.float8_e4m3fn_x4
ADD = mybir.AluOpType.add
MIN = mybir.AluOpType.min
MULT = mybir.AluOpType.mult
IS_GE = mybir.AluOpType.is_ge
EXP = mybir.ActivationFunctionType.Exp
COPY = mybir.ActivationFunctionType.Copy

P = 128
PACK = 4
ROWS = 512
T = 512
U = 128
K = 512
ROW_TILES = ROWS // P
K_TILES = K // P
IDLE_PASSES = 3
WARM_UP_PASSES = 12
EARLY_TILES = 2

FLOPS = 2 * (ROWS * T * U + ROWS * T * K + U * ROWS * K)


def tile_swd_s_kernel(tc, x1, x2, w1, b1, w2, b2, global_att, i, j, out):
    nc = tc.nc
    half_window = (6 + i) // 2 - 1
    assert K % (6 + i) == 0

    with tc.tile_pool(name="keep", bufs=1) as keep, tc.psum_pool(
        name="psum", bufs=6
    ) as psum, tc.manual_schedule():
        x1_sb = keep.tile([P, ROW_TILES, T], BF16)
        x2_sb = keep.tile([P, ROW_TILES, T], BF16)
        w1_sb = keep.tile([P, 1, T], BF16)
        w2_sb = keep.tile([P, K_TILES, T], BF16)
        ga_sb = keep.tile([P, K_TILES, U], BF16)
        x1_rows = x1.rearrange("(p j) t -> p j t", j=ROW_TILES)
        x2_rows = x2.rearrange("(p j) t -> p j t", j=ROW_TILES)
        nc.sync.dma_start(out=x1_sb[:, 0, :], in_=x1_rows[:, 0, :])
        nc.sync.dma_start(out=x1_sb[:, 1, :], in_=x1_rows[:, 1, :])
        nc.sync.dma_start(out=x1_sb[:, 2:4, :], in_=x1_rows[:, 2:4, :])
        nc.sync.dma_start(out=w1_sb[:, 0, :], in_=w1)
        nc.sync.dma_start(out=x2_sb[:, 0:2, :], in_=x2_rows[:, 0:2, :])
        nc.sync.dma_start(out=x2_sb[:, 2:4, :], in_=x2_rows[:, 2:4, :])
        for m in range(K_TILES):
            nc.sync.dma_start(out=w2_sb[:, m, :], in_=w2[m * P : (m + 1) * P, :])
        nc.sync.dma_start(out=ga_sb[:], in_=global_att.rearrange("(m p) u -> p m u", p=P))

        bias_rows = keep.tile([P, K + U], BF16)
        nc.scalar.dma_start(out=bias_rows[P - 1 : P, K : K + U], in_=b1.rearrange("(o u) -> o u", o=1))
        nc.scalar.dma_start(out=bias_rows[P - 1 : P, 0:K], in_=b2.rearrange("(o k) -> o k", o=1))
        ones = keep.tile([P, P], BF16)
        zeros = keep.tile([P, P * PACK], BF16, align_bytes=64)
        zero_codes = keep.tile([P, P], U32, align_bytes=64)
        zero_scales = keep.tile([P, P], U8, align_bytes=64)
        nc.vector.memset(zeros[:].bitcast(U32), 0)
        nc.vector.memset(ones[:], 1.0)
        nc.vector.quantize_mx(out=zero_codes[:].bitcast(FP8X4), scales=zero_scales[:], in_=zeros[:])
        nc.vector.memset(bias_rows[0 : P - 1, :].bitcast(U32), 0)
        exp_in = keep.tile([P, 1], F32)
        exp_out = keep.tile([P, 1], F32)
        nc.vector.memset(exp_in[:], 0.0)
        nc.scalar.activation(out=exp_out[:], in_=exp_in[:], func=EXP)
        ident_f32 = keep.tile([P, P], F32)
        masks.make_identity(nc, ident_f32[:])
        reach = half_window + 1
        band_cols = P + 2 * reach
        band = keep.tile([P, band_cols], F32)
        nc.gpsimd.memset(band[:], 1.0)
        nc.gpsimd.affine_select(
            out=band[:], in_=band[:], pattern=[[1, band_cols]], compare_op=IS_GE, fill=0.0,
            base=half_window - reach, channel_multiplier=-1,
        )
        nc.gpsimd.affine_select(
            out=band[:], in_=band[:], pattern=[[-1, band_cols]], compare_op=IS_GE, fill=0.0,
            base=reach + half_window, channel_multiplier=1,
        )

        warm_bank = psum.tile([P, P], F32, tag="work")
        for i in range(WARM_UP_PASSES):
            nc.tensor.matmul_mx(
                out=warm_bank[:],
                lhsT=zero_codes[:].bitcast(FP8X4),
                lhsT_scale=zero_scales[:],
                rhs=zero_codes[:].bitcast(FP8X4),
                rhs_scale=zero_scales[:],
                start=True,
                stop=True,
            )
        b1_bank = psum.tile([P, U], F32, tag="work")
        b2_bank = psum.tile([P, K], F32, tag="work")
        nc.tensor.matmul(out=b1_bank[:], lhsT=ones[:], rhs=bias_rows[:, K : K + U], start=True, stop=True)
        nc.tensor.matmul(out=b2_bank[:], lhsT=ones[:], rhs=bias_rows[:, 0:K], start=True, stop=True)
        b1_all = keep.tile([P, U], F32)
        b2_all = keep.tile([P, K], F32)
        nc.vector.tensor_copy(out=b1_all[:], in_=b1_bank[:])
        nc.vector.tensor_copy(out=b2_all[:], in_=b2_bank[:])

        x1_grouped = keep.tile([P, ROW_TILES, P, PACK], BF16, align_bytes=64)
        x2_grouped = keep.tile([P, ROW_TILES, P, PACK], BF16, align_bytes=64)
        w1_grouped = keep.tile([P, 1, P, PACK], BF16, align_bytes=64)
        w2_grouped = keep.tile([P, K_TILES, P, PACK], BF16, align_bytes=64)
        a_grouped = keep.tile([P, U, PACK], BF16, align_bytes=64)
        c_grouped = keep.tile([P, K_TILES, P, PACK], BF16, align_bytes=64)
        x1_codes = keep.tile([P, ROWS], U32, align_bytes=64)
        x2_codes = keep.tile([P, ROWS], U32, align_bytes=64)
        w1_codes = keep.tile([P, U], U32, align_bytes=64)
        w2_codes = keep.tile([P, K], U32, align_bytes=64)
        a_codes = keep.tile([P, U], U32, align_bytes=64)
        c_codes = keep.tile([P, K], U32, align_bytes=64)
        x1_scales = keep.tile([P, ROWS], U8, align_bytes=64)
        x2_scales = keep.tile([P, ROWS], U8, align_bytes=64)
        w1_scales = keep.tile([P, U], U8, align_bytes=64)
        w2_scales = keep.tile([P, K], U8, align_bytes=64)
        a_scales = keep.tile([P, U], U8, align_bytes=64)
        c_scales = keep.tile([P, K], U8, align_bytes=64)

        def flip(rows_sb, grouped, i, copy):
            words = rows_sb[:, i, :].bitcast(F32)
            flipped = psum.tile([P, 2, P], F32, tag="work")
            for h in range(2):
                nc.tensor.transpose(flipped[:, h, :], words[:, h * P : (h + 1) * P], ident_f32[:])
            copy(out=grouped[:, i, :, :].bitcast(F32), in_=flipped[:].rearrange("q h r -> q r h"))

        def quantise(grouped, codes, scales, first, count):
            cols = slice(first * P, (first + count) * P)
            nc.vector.quantize_mx(
                out=codes[:, cols].bitcast(FP8X4),
                scales=scales[:, cols],
                in_=grouped[:, first : first + count, :, :].rearrange("q i r v -> q (i r v)"),
            )

        def product_bank(x_codes, x_scales, w_codes, w_scales):
            bank = psum.tile([P, ROW_TILES, P], F32, tag="work")
            for jj in range(ROW_TILES):
                tile_cols = slice(jj * P, (jj + 1) * P)
                nc.tensor.matmul_mx(
                    out=bank[:, jj, :],
                    lhsT=x_codes[:, tile_cols].bitcast(FP8X4),
                    lhsT_scale=x_scales[:, tile_cols],
                    rhs=w_codes.bitcast(FP8X4),
                    rhs_scale=w_scales,
                    start=True,
                    stop=True,
                )
            return bank

        def add_bias(bank, bias, grouped):
            nc.vector.tensor_tensor(
                out=grouped,
                in0=bank[:].rearrange("p j s -> p s j"),
                in1=bias.unsqueeze(2).to_broadcast([P, P, PACK]),
                op=ADD,
            )

        def c_product(m):
            k_cols = slice(m * P, (m + 1) * P)
            return product_bank(x2_codes, x2_scales, w2_codes[:, k_cols], w2_scales[:, k_cols])

        def c_bias(m, bank):
            add_bias(bank, b2_all[:, m * P : (m + 1) * P], c_grouped[:, m, :, :])

        def quantise_c(m):
            quantise(c_grouped, c_codes, c_scales, m, 1)

        def quantise_a():
            nc.vector.quantize_mx(
                out=a_codes[:].bitcast(FP8X4), scales=a_scales[:], in_=a_grouped[:].rearrange("p s j -> p (s j)")
            )

        on_scalar, on_vector = nc.scalar.copy, nc.vector.tensor_copy
        flip(x1_sb, x1_grouped, 0, on_scalar)
        flip(x1_sb, x1_grouped, 1, on_scalar)
        quantise(x1_grouped, x1_codes, x1_scales, 0, 1)
        flip(x1_sb, x1_grouped, 2, on_scalar)
        quantise(x1_grouped, x1_codes, x1_scales, 1, 1)
        flip(x1_sb, x1_grouped, 3, on_vector)
        flip(w1_sb, w1_grouped, 0, on_scalar)
        quantise(x1_grouped, x1_codes, x1_scales, 2, 1)
        flip(x2_sb, x2_grouped, 0, on_scalar)
        quantise(x1_grouped, x1_codes, x1_scales, 3, 1)
        flip(x2_sb, x2_grouped, 1, on_scalar)
        quantise(w1_grouped, w1_codes, w1_scales, 0, 1)
        flip(x2_sb, x2_grouped, 2, on_scalar)
        quantise(x2_grouped, x2_codes, x2_scales, 0, 1)
        flip(x2_sb, x2_grouped, 3, on_scalar)
        quantise(x2_grouped, x2_codes, x2_scales, 1, 1)
        flip(w2_sb, w2_grouped, 0, on_scalar)
        quantise(x2_grouped, x2_codes, x2_scales, 2, 1)
        flip(w2_sb, w2_grouped, 1, on_scalar)
        quantise(x2_grouped, x2_codes, x2_scales, 3, 1)
        a_bank = product_bank(x1_codes, x1_scales, w1_codes[:], w1_scales[:])
        quantise(w2_grouped, w2_codes, w2_scales, 0, 1)
        flip(w2_sb, w2_grouped, 2, on_scalar)
        add_bias(a_bank, b1_all[:], a_grouped[:])
        flip(w2_sb, w2_grouped, 3, on_scalar)
        quantise(w2_grouped, w2_codes, w2_scales, 1, 1)
        quantise(w2_grouped, w2_codes, w2_scales, 2, 1)
        quantise_a()
        quantise(w2_grouped, w2_codes, w2_scales, 3, 1)
        c_banks = [c_product(m) for m in range(K_TILES)]
        c_bias(0, c_banks[0])
        c_bias(1, c_banks[1])
        quantise_c(0)
        c_bias(2, c_banks[2])
        quantise_c(1)
        c_bias(3, c_banks[3])
        quantise_c(2)
        quantise_c(3)

        early_cols = EARLY_TILES * P - reach
        late_origin = (EARLY_TILES - 1) * P
        ga_f32 = keep.tile([P, K_TILES, U], F32)
        nc.scalar.copy(out=ga_f32[:], in_=ga_sb[:])
        early_bank = psum.tile([P, EARLY_TILES * P], F32, tag="early", bufs=1)
        late_bank = psum.tile([P, K - late_origin], F32, tag="late", bufs=1)

        def lay_global_att(bank, origin, m, first):
            nc.tensor.matmul(
                out=bank[:, m * P - origin : (m + 1) * P - origin],
                lhsT=ga_f32[:, m, :],
                rhs=ident_f32[:],
                is_transpose=True,
                start=first,
                stop=False,
            )

        ti_t = keep.tile([P, K_TILES, U], F32)

        def ti_product(m):
            k_cols = slice(m * P, (m + 1) * P)
            ti_t_bank = psum.tile([P, U], F32, tag="work")
            nc.tensor.matmul_mx(
                out=ti_t_bank[:],
                lhsT=c_codes[:, k_cols].bitcast(FP8X4),
                lhsT_scale=c_scales[:, k_cols],
                rhs=a_codes[:].bitcast(FP8X4),
                rhs_scale=a_scales[:],
                start=True,
                stop=True,
            )
            nc.scalar.copy(out=ti_t[:, m, :], in_=ti_t_bank[:])

        ti_product(0)
        for m in range(EARLY_TILES):
            lay_global_att(early_bank, 0, m, m == 0)
        for m in range(EARLY_TILES - 1, K_TILES):
            lay_global_att(late_bank, late_origin, m, m == EARLY_TILES - 1)

        def spread(bank, origin, m, low, high, last):
            window = m * P - reach
            nc.tensor.matmul(
                out=bank[:, low - origin : high - origin],
                lhsT=ti_t[:, m, :],
                rhs=band[:, low - window : high - window],
                start=False,
                stop=last,
            )

        neg_logits = keep.tile([P, K], F32)
        neg_max_early = keep.tile([P, 1], F32)
        neg_max = keep.tile([P, 1], F32)

        def spread_tile(m):
            low = max(m * P - reach, 0)
            high = min((m + 1) * P + reach, K)
            if low < early_cols:
                spread(early_bank, 0, m, low, min(high, early_cols), high > early_cols)
            if high > early_cols:
                spread(late_bank, late_origin, m, max(low, early_cols), high, m == K_TILES - 1)

        ti_product(1)
        spread_tile(0)
        ti_product(2)
        ti_product(3)
        spread_tile(1)
        nc.vector.tensor_scalar(
            out=neg_logits[:, 0:early_cols], in0=early_bank[:, 0:early_cols], scalar1=-1.0,
            scalar2=None, op0=MULT, op1=MIN, accum_out=neg_max_early[:, 0:1],
        )
        spread_tile(2)
        spread_tile(3)

        for i in range(IDLE_PASSES):
            idle_bank = psum.tile([P, K], F32, tag="work")
            nc.tensor.matmul_mx(
                out=idle_bank[:],
                lhsT=c_codes[:, 0:P].bitcast(FP8X4),
                lhsT_scale=c_scales[:, 0:P],
                rhs=c_codes[:].bitcast(FP8X4),
                rhs_scale=c_scales[:],
                start=True,
                stop=True,
            )

        exp_sum = keep.tile([P, 1], F32)
        inv_sum = keep.tile([P, 1], F32)
        expd = keep.tile([P, K], F32)
        prob = keep.tile([P, K], F32)
        nc.vector.tensor_scalar(
            out=neg_logits[:, early_cols:K], in0=late_bank[:, early_cols - late_origin : K - late_origin],
            scalar1=-1.0, scalar2=neg_max_early[:, 0:1], op0=MULT, op1=MIN, accum_out=neg_max[:, 0:1],
        )
        nc.scalar.activation(
            out=expd[:], in_=neg_logits[:], func=EXP, bias=neg_max[:, 0:1], scale=-1.0,
            accum_out=exp_sum[:, 0:1],
        )
        nc.vector.reciprocal(out=inv_sum[:], in_=exp_sum[:])

        out_sb = keep.tile([P, K_TILES, U], F32)
        out_rows = out.rearrange("(m p) u -> p m u", p=P)
        nc.vector.tensor_scalar_mul(out=prob[:, 0:P], in0=expd[:, 0:P], scalar1=inv_sum[:, 0:1])
        nc.scalar.activation(out=prob[:, 3 * P : K], in_=expd[:, 3 * P : K], func=COPY, scale=inv_sum[:, 0:1])
        nc.vector.tensor_scalar_mul(out=prob[:, P : 3 * P], in0=expd[:, P : 3 * P], scalar1=inv_sum[:, 0:1])
        for m in range(K_TILES):
            out_bank = psum.tile([P, U], F32, tag="work")
            nc.tensor.transpose(out_bank[:], prob[:, m * P : (m + 1) * P], ident_f32[:])
            if m % 2 == 0:
                nc.vector.tensor_copy(out=out_sb[:, m, :], in_=out_bank[:])
            else:
                nc.scalar.copy(out=out_sb[:, m, :], in_=out_bank[:])
        for half in range(2):
            tiles = slice(2 * half, 2 * half + 2)
            nc.sync.dma_start(out=out_rows[:, tiles, :], in_=out_sb[:, tiles, :])
